import numpy as np
import ml_dtypes


BF16 = ml_dtypes.bfloat16


def bf(x):
    return np.asarray(x, np.float32).astype(BF16)


def f64(x):
    return np.asarray(x).astype(np.float64)


E2M1 = np.array([0.0, 0.5, 1.0, 1.5, 2.0, 3.0, 4.0, 6.0, -0.0, -0.5, -1.0, -1.5, -2.0, -3.0, -4.0, -6.0])


def pack_weight(w, fmt):
    k, n = w.shape
    w = f64(bf(w)).reshape(k // 32, 32, n)
    amax = np.abs(w).max(1)
    if fmt == "e4m3":
        byte = np.frexp(amax)[1] - 1 + 127 - 7
    else:
        mant, ex = np.frexp(amax / 6.0)
        byte = np.where(mant > 0.5, ex, ex - 1) + 127
    byte = np.clip(np.where(amax > 0, byte, 1), 1, 254)
    scaled = (w * np.exp2(127.0 - byte)[:, None, :]).reshape(k, n).astype(np.float32)
    by_word = np.ascontiguousarray(scaled.reshape(k // 512, 128, 4, n).transpose(0, 1, 3, 2))
    if fmt == "e4m3":
        words = by_word.astype(ml_dtypes.float8_e4m3fn).view(np.uint8)
    else:
        c = by_word.astype(ml_dtypes.float4_e2m1fn).view(np.uint8) & 0xF
        words = c[..., 0::2] | (c[..., 1::2] << 4)
    return np.ascontiguousarray(words), np.ascontiguousarray(byte.astype(np.uint8).reshape(k // 512, 16, n))


def unpack_weight(words, scales, fmt):
    g, p, n, _ = words.shape
    if fmt == "e4m3":
        vals = np.ascontiguousarray(words).view(ml_dtypes.float8_e4m3fn).astype(np.float64)
    else:
        nib = np.empty((g, p, n, 4), np.uint8)
        nib[..., 0::2] = words & 0xF
        nib[..., 1::2] = words >> 4
        vals = E2M1[nib]
    vals = vals * np.repeat(np.exp2(scales.astype(np.float64) - 127.0), 8, axis=1)[..., None]
    return vals.transpose(0, 1, 3, 2).reshape(g * 512, n)

def pack4(w):
    words, scales = pack_weight(w, "e2m1")
    return words.reshape(words.shape[0], 128, -1), scales


def unpack4(words, scales):
    return unpack_weight(words.reshape(words.shape[0], 128, -1, 2), scales, "e2m1")


def kspread(k):
    return np.exp2(np.repeat(np.random.randint(-6, 7, k // 32), 32).astype(np.float64))


B, L, D, H, DH = 4, 256, 8192, 16, 64
THETA = 100000.0
E = H * DH


def rope(t):
    pos = np.arange(L, dtype=np.float64)
    inv_freq = 1.0 / THETA ** (np.arange(0, DH, 2, dtype=np.float64) / DH)
    ang = pos[:, None] * inv_freq[None, :]
    cos = np.cos(ang)[:, :, None]
    sin = np.sin(ang)[:, :, None]
    tp = t.reshape(*t.shape[:-1], DH // 2, 2)
    x1, x2 = tp[..., 0], tp[..., 1]
    rot = np.stack([-x2, x1], axis=-1)
    out = tp * cos + rot * sin
    return out.reshape(*t.shape)


def setup_inputs():
    s = kspread(D)
    x = np.random.standard_normal((B, L, D)) * s
    w = np.random.standard_normal((3 * E, D)) / np.sqrt(D) / s
    x_words, x_scales = pack4(np.ascontiguousarray(x.reshape(B * L, D).T))
    words, scales = pack4(np.ascontiguousarray(w.T))
    return {"x_words": x_words, "x_scales": x_scales, "W_words": words, "W_scales": scales}


def reference(x_words, x_scales, W_words, W_scales):
    xv = unpack4(x_words, x_scales).T.reshape(B, L, D)
    qkv = xv @ unpack4(W_words, W_scales)
    qkv = qkv.reshape(B, L, 3, H, DH)
    qkv = np.transpose(qkv, (0, 3, 1, 2, 4))
    q, k, v = qkv[..., 0, :], qkv[..., 1, :], qkv[..., 2, :]
    return rope(q), rope(k), np.ascontiguousarray(v)

@@ -1,0 +1,241 @@
+from contextlib import ExitStack
+import math
+
+import concourse.mybir as mybir
+
+F32 = mybir.dt.float32
+BF16 = mybir.dt.bfloat16
+I32 = mybir.dt.int32
+U8 = mybir.dt.uint8
+FP4X4 = mybir.dt.float4_e2m1fn_x4
+ALU = mybir.AluOpType
+ACT = mybir.ActivationFunctionType
+
+B, L, D, H, DH = 4, 256, 8192, 16, 64
+THETA = 100000.0
+P = 128
+PASSES = D // 512
+TOKENS = B * L
+TOKEN_TILES = TOKENS // P
+N_TILE = 512
+HEADS_PER_BLOCK = N_TILE // DH
+COL_BLOCKS = 3 * H * DH // N_TILE
+PAIRS = DH // 2
+
+FLOPS = 2 * TOKENS * D * 3 * H * DH
+
+FIRST_RUNS = ((0, 2), (2, 6), (6, 11), (11, 16))
+CHUNK = 4
+WARM_MATMULS = 6
+
+
+def tile_multiheadselfattention_pa_kernel(
+    tc, x_words, x_scales, W_words, W_scales, out_0, out_1, out_2
+):
+    nc = tc.nc
+    outs = (out_0, out_1, out_2)
+
+    with ExitStack() as ctx:
+        keep = ctx.enter_context(tc.tile_pool(name="keep", bufs=1))
+        work = ctx.enter_context(tc.tile_pool(name="work", bufs=4))
+        psum = ctx.enter_context(tc.psum_pool(name="psum", bufs=8))
+        ctx.enter_context(tc.manual_schedule())
+
+        x_code = []
+        for g in range(PASSES):
+            xc = keep.tile([P, 2 * TOKENS], U8, name="xc%d" % g, align_bytes=64)
+            x_code.append(xc)
+        x_plane = [None] * PASSES
+        w_plane = [[None] * PASSES for c in range(COL_BLOCKS)]
+        w_code = [[None] * PASSES for c in range(COL_BLOCKS)]
+        x_plane_tiles = []
+        w_plane_tiles = []
+        for r, (g0, g1) in enumerate(FIRST_RUNS):
+            xp = keep.tile([P, g1 - g0, TOKENS], U8, name="xp%d" % r, align_bytes=64)
+            wp = keep.tile([P, g1 - g0, N_TILE], U8, name="wp0_%d" % r, align_bytes=64)
+            x_plane_tiles.append(xp)
+            w_plane_tiles.append((0, g0, g1, wp))
+            for g in range(g0, g1):
+                x_plane[g] = xp[:, g - g0, :]
+                w_plane[0][g] = wp[:, g - g0, :]
+        for g in range(PASSES):
+            wc = keep.tile([P, 2 * N_TILE], U8, name="wc0_%d" % g, align_bytes=64)
+            w_code[0][g] = wc[:, :]
+        w_chunks = []
+        for c in range(1, COL_BLOCKS):
+            wp = keep.tile([P, PASSES, N_TILE], U8, name="wp%d" % c, align_bytes=64)
+            w_plane_tiles.append((c, 0, PASSES, wp))
+            for g in range(PASSES):
+                w_plane[c][g] = wp[:, g, :]
+            for g0 in range(0, PASSES, CHUNK):
+                wc = keep.tile([P, CHUNK, 2 * N_TILE], U8, name="wc%d_%d" % (c, g0), align_bytes=64)
+                w_chunks.append((c, g0, wc))
+                for g in range(g0, g0 + CHUNK):
+                    w_code[c][g] = wc[:, g - g0, :]
+
+        warm = keep.tile([P, N_TILE], BF16, name="warm")
+        nc.gpsimd.memset(warm[:, :], 0.0)
+        pos_i = keep.tile([P, 2], I32, name="pos_i")
+        nc.gpsimd.iota(pos_i[:, :], pattern=[[P, 2]], base=0, channel_multiplier=1)
+
+        for r in range(len(FIRST_RUNS)):
+            nc.vector.memset(x_plane_tiles[r][:, :, :].bitcast(I32), 0)
+            nc.vector.memset(w_plane_tiles[r][3][:, :, :].bitcast(I32), 0)
+        for c, g0, g1, wp in w_plane_tiles[len(FIRST_RUNS):]:
+            nc.vector.memset(wp[:, :, :].bitcast(I32), 0)
+
+        def load_x_scales(r):
+            g0, g1 = FIRST_RUNS[r]
+            for q in range(4):
+                nc.sync.dma_start(
+                    out=x_plane_tiles[r][32 * q : 32 * q + 4, :, :].bitcast(I32),
+                    in_=x_scales[g0:g1, 4 * q : 4 * q + 4, :].rearrange("g r n -> r g n").bitcast(I32),
+                )
+
+        def load_w_scales(entry):
+            c, g0, g1, wp = entry
+            for q in range(4):
+                nc.sync.dma_start(
+                    out=wp[32 * q : 32 * q + 4, :, :].bitcast(I32),
+                    in_=W_scales[g0:g1, 4 * q : 4 * q + 4, c * N_TILE : (c + 1) * N_TILE]
+                    .rearrange("g r n -> r g n")
+                    .bitcast(I32),
+                )
+
+        def load_first_codes(g):
+            nc.sync.dma_start(out=x_code[g][:, :].bitcast(I32), in_=x_words[g].bitcast(I32))
+            nc.sync.dma_start(out=w_code[0][g].bitcast(I32), in_=W_words[g, :, 0 : 2 * N_TILE].bitcast(I32))
+
+        load_first_codes(0)
+        for r, (g0, g1) in enumerate(FIRST_RUNS):
+            load_x_scales(r)
+            load_w_scales(w_plane_tiles[r])
+            for g in range(max(g0, 1), g1):
+                load_first_codes(g)
+        for c in range(1, COL_BLOCKS):
+            load_w_scales(w_plane_tiles[len(FIRST_RUNS) + c - 1])
+            for cc, g0, wc in w_chunks:
+                if cc == c:
+                    nc.sync.dma_start(
+                        out=wc[:, :, :].bitcast(I32),
+                        in_=W_words[g0 : g0 + CHUNK, :, 2 * N_TILE * c : 2 * N_TILE * (c + 1)]
+                        .rearrange("g p n -> p g n")
+                        .bitcast(I32),
+                    )
+
+        dummy = psum.tile([P, N_TILE], F32, tag="acc", name="dummy")
+        for i in range(WARM_MATMULS):
+            nc.tensor.matmul(out=dummy[:, :], lhsT=warm[:, 0:P], rhs=warm[:, :], start=True, stop=True)
+
+        pos = keep.tile([P, 2], F32, name="pos")
+        nc.vector.tensor_copy(out=pos[:, :], in_=pos_i[:, :])
+        t_hi = keep.tile([P, 2, PAIRS], F32, name="t_hi")
+        t_lo = keep.tile([P, 2, PAIRS], F32, name="t_lo")
+        for i in range(PAIRS):
+            turns = THETA ** (-2.0 * i / DH) / (2.0 * math.pi)
+            hi = round(turns * 131072.0) / 131072.0
+            lo = turns - hi
+            nc.vector.tensor_scalar(out=t_hi[:, :, i], in0=pos[:, :], scalar1=hi, scalar2=None, op0=ALU.mult)
+            nc.vector.tensor_scalar(out=t_lo[:, :, i], in0=pos[:, :], scalar1=lo, scalar2=None, op0=ALU.mult)
+        W2 = 2 * PAIRS
+        hi_flat = t_hi[:, :, :].rearrange("p a i -> p (a i)")
+        lo_flat = t_lo[:, :, :].rearrange("p a i -> p (a i)")
+        k_i = keep.tile([P, W2], I32, name="k_i")
+        k_f = keep.tile([P, W2], F32, name="k_f")
+        fr = keep.tile([P, W2], F32, name="fr")
+        fr1 = keep.tile([P, W2], F32, name="fr1")
+        fr2 = keep.tile([P, W2], F32, name="fr2")
+        fc = keep.tile([P, W2], F32, name="fc")
+        ysn = keep.tile([P, W2], F32, name="ysn")
+        ycn = keep.tile([P, W2], F32, name="ycn")
+        nc.vector.tensor_copy(out=k_i[:, :], in_=hi_flat)
+        nc.vector.tensor_copy(out=k_f[:, :], in_=k_i[:, :])
+        nc.vector.tensor_tensor(out=fr[:, :], in0=hi_flat, in1=k_f[:, :], op=ALU.subtract)
+        nc.vector.scalar_tensor_tensor(out=fr1[:, :], in0=fr[:, :], scalar=0.0, in1=fr[:, :], op0=ALU.is_lt, op1=ALU.add)
+        nc.vector.tensor_tensor(out=fr2[:, :], in0=fr1[:, :], in1=lo_flat, op=ALU.add)
+        nc.vector.scalar_tensor_tensor(out=ysn[:, :], in0=fr2[:, :], scalar=0.5, in1=fr2[:, :], op0=ALU.is_gt, op1=ALU.subtract)
+        nc.vector.tensor_scalar(out=fc[:, :], in0=fr2[:, :], scalar1=0.25, scalar2=None, op0=ALU.add)
+        nc.vector.scalar_tensor_tensor(out=ycn[:, :], in0=fc[:, :], scalar=0.5, in1=fc[:, :], op0=ALU.is_gt, op1=ALU.subtract)
+
+        cos_t = keep.tile([P, 2, PAIRS, 2], F32, name="cos_t")
+        sin_t = keep.tile([P, 2, PAIRS, 2], F32, name="sin_t")
+        ysn3 = ysn[:, :].rearrange("p (a i) -> p a i", a=2)
+        ycn3 = ycn[:, :].rearrange("p (a i) -> p a i", a=2)
+        two_pi = 2.0 * math.pi
+        nc.scalar.activation(out=sin_t[:, :, :, 0], in_=ysn3, func=ACT.Sin, scale=-two_pi)
+        nc.scalar.activation(out=sin_t[:, :, :, 1], in_=ysn3, func=ACT.Sin, scale=two_pi)
+        nc.scalar.activation(out=cos_t[:, :, :, 0], in_=ycn3, func=ACT.Sin, scale=-two_pi)
+        nc.scalar.activation(out=cos_t[:, :, :, 1], in_=ycn3, func=ACT.Sin, scale=-two_pi)
+
+        def mx_pass(acc, g, m, c, col0, width):
+            nc.tensor.matmul_mx(
+                out=acc,
+                lhsT=x_code[g][:, 2 * P * m : 2 * P * (m + 1)].bitcast(FP4X4),
+                lhsT_scale=x_plane[g][:, P * m : P * (m + 1)],
+                rhs=w_code[c][g][:, 2 * col0 : 2 * (col0 + width)].bitcast(FP4X4),
+                rhs_scale=w_plane[c][g][:, col0 : col0 + width],
+                start=(g == 0),
+                stop=(g == PASSES - 1),
+            )
+
+        def dest(m, c, col0, width):
+            part = c // 2
+            h0 = (c % 2) * HEADS_PER_BLOCK + col0 // DH
+            b = m // 2
+            l0 = (m % 2) * P
+            return outs[part][b, h0 : h0 + width // DH, l0 : l0 + P, :].rearrange("h l d -> l h d")
+
+        def rope(acc, m, c):
+            a = m % 2
+            heads = HEADS_PER_BLOCK
+            cos_b = cos_t[:, a, :, :].rearrange("p i e -> p (i e)").unsqueeze(1).to_broadcast([P, heads, DH])
+            sin_b = sin_t[:, a, :, :].rearrange("p i e -> p (i e)").unsqueeze(1).to_broadcast([P, heads, DH])
+            acc3 = acc.rearrange("p (h d) -> p h d", h=heads)
+            t1 = work.tile([P, N_TILE], F32, tag="t1", bufs=6, name="t1")
+            t2 = work.tile([P, N_TILE], F32, tag="t2", bufs=3, name="t2")
+            nc.vector.tensor_tensor(out=t1[:, :].rearrange("p (h d) -> p h d", h=heads), in0=acc3, in1=cos_b, op=ALU.mult)
+            nc.vector.tensor_tensor(out=t2[:, :].rearrange("p (h d) -> p h d", h=heads), in0=acc3, in1=sin_b, op=ALU.mult)
+            nc.vector.tensor_tensor(
+                out=t1[:, :].rearrange("p (n e) -> p n e", e=2),
+                in0=t1[:, :].rearrange("p (n e) -> p n e", e=2),
+                in1=t2[:, :].rearrange("p (n e) -> p n e", e=2)[:, :, ::-1],
+                op=ALU.add,
+            )
+            nc.scalar.dma_start(out=dest(m, c, 0, N_TILE), in_=t1[:, :].rearrange("p (h d) -> p h d", h=heads))
+
+        def plain(acc, m, c, col0, width, turn):
+            v = work.tile([P, width], F32, tag="v", bufs=4, name="v")
+            src = v[:, :].rearrange("p (h d) -> p h d", d=DH)
+            if turn % 2 == 0:
+                nc.scalar.copy(out=v[:, :], in_=acc)
+                nc.scalar.dma_start(out=dest(m, c, col0, width), in_=src)
+            else:
+                nc.vector.tensor_copy(out=v[:, :], in_=acc)
+                nc.sync.dma_start(out=dest(m, c, col0, width), in_=src)
+
+        accs = []
+        for m in range(TOKEN_TILES):
+            acc = psum.tile([P, N_TILE], F32, tag="acc", name="acc")
+            accs.append(acc)
+        for g in range(PASSES):
+            for m in range(TOKEN_TILES):
+                mx_pass(accs[m][:, :], g, m, 0, 0, N_TILE)
+        for m in range(TOKEN_TILES):
+            rope(accs[m][:, :], m, 0)
+
+        groups = []
+        for c in range(1, COL_BLOCKS):
+            for m in range(TOKEN_TILES):
+                if c == COL_BLOCKS - 1 and m == TOKEN_TILES - 1:
+                    groups.append((m, c, 0, N_TILE // 2))
+                    groups.append((m, c, N_TILE // 2, N_TILE // 2))
+                else:
+                    groups.append((m, c, 0, N_TILE))
+        for turn, (m, c, col0, width) in enumerate(groups):
+            acc = psum.tile([P, width], F32, tag="acc", name="acc")
+            for g in range(PASSES):
+                mx_pass(acc[:, :], g, m, c, col0, width)
+            if c < 4:
+                rope(acc[:, :], m, c)
+            else:
+                plain(acc[:, :], m, c, col0, width, turn)

@@ -191,6 +191,9 @@ def tile_multiheadselfattention_pa_kernel(
             cos_b = cos_t[:, a, :, :].rearrange("p i e -> p (i e)").unsqueeze(1).to_broadcast([P, heads, DH])
             sin_b = sin_t[:, a, :, :].rearrange("p i e -> p (i e)").unsqueeze(1).to_broadcast([P, heads, DH])
             acc3 = acc.rearrange("p (h d) -> p h d", h=heads)
+            u = work.tile([P, N_TILE], F32, tag="u", bufs=3, name="u")
+            nc.scalar.copy(out=u[:, :], in_=acc)
+            acc3 = u[:, :].rearrange("p (h d) -> p h d", h=heads)
             t1 = work.tile([P, N_TILE], F32, tag="t1", bufs=6, name="t1")
             t2 = work.tile([P, N_TILE], F32, tag="t2", bufs=3, name="t2")
             nc.vector.tensor_tensor(out=t1[:, :].rearrange("p (h d) -> p h d", h=heads), in0=acc3, in1=cos_b, op=ALU.mult)

@@ -27,6 +27,7 @@ FLOPS = 2 * TOKENS * D * 3 * H * DH
 FIRST_RUNS = ((0, 2), (2, 6), (6, 11), (11, 16))
 CHUNK = 4
 WARM_MATMULS = 6
+HEAD_TILES = 4
 
 
 def tile_multiheadselfattention_pa_kernel(
@@ -45,6 +46,7 @@ def tile_multiheadselfattention_pa_kernel(
         for g in range(PASSES):
             xc = keep.tile([P, 2 * TOKENS], U8, name="xc%d" % g, align_bytes=64)
             x_code.append(xc)
+        x_head = keep.tile([P, 2 * P * HEAD_TILES], U8, name="x_head", align_bytes=64)
         x_plane = [None] * PASSES
         w_plane = [[None] * PASSES for c in range(COL_BLOCKS)]
         w_code = [[None] * PASSES for c in range(COL_BLOCKS)]
@@ -73,6 +75,7 @@ def tile_multiheadselfattention_pa_kernel(
                 for g in range(g0, g0 + CHUNK):
                     w_code[c][g] = wc[:, g - g0, :]
 
+        nc.gpsimd.memset(w_plane_tiles[0][3][:, :, :].bitcast(F32), 0.0)
         warm = keep.tile([P, N_TILE], BF16, name="warm")
         nc.gpsimd.memset(warm[:, :], 0.0)
         pos_i = keep.tile([P, 2], I32, name="pos_i")
@@ -80,7 +83,8 @@ def tile_multiheadselfattention_pa_kernel(
 
         for r in range(len(FIRST_RUNS)):
             nc.vector.memset(x_plane_tiles[r][:, :, :].bitcast(I32), 0)
-            nc.vector.memset(w_plane_tiles[r][3][:, :, :].bitcast(I32), 0)
+            if r > 0:
+                nc.vector.memset(w_plane_tiles[r][3][:, :, :].bitcast(I32), 0)
         for c, g0, g1, wp in w_plane_tiles[len(FIRST_RUNS):]:
             nc.vector.memset(wp[:, :, :].bitcast(I32), 0)
 
@@ -106,10 +110,16 @@ def tile_multiheadselfattention_pa_kernel(
             nc.sync.dma_start(out=x_code[g][:, :].bitcast(I32), in_=x_words[g].bitcast(I32))
             nc.sync.dma_start(out=w_code[0][g].bitcast(I32), in_=W_words[g, :, 0 : 2 * N_TILE].bitcast(I32))
 
-        load_first_codes(0)
+        head_bytes = 2 * P * HEAD_TILES
+        nc.sync.dma_start(out=x_head[:, :].bitcast(I32), in_=x_words[0, :, 0:head_bytes].bitcast(I32))
+        nc.sync.dma_start(out=w_code[0][0].bitcast(I32), in_=W_words[0, :, 0 : 2 * N_TILE].bitcast(I32))
         for r, (g0, g1) in enumerate(FIRST_RUNS):
-            load_x_scales(r)
             load_w_scales(w_plane_tiles[r])
+            load_x_scales(r)
+            if r == 0:
+                nc.sync.dma_start(
+                    out=x_code[0][:, head_bytes:].bitcast(I32), in_=x_words[0, :, head_bytes:].bitcast(I32)
+                )
             for g in range(max(g0, 1), g1):
                 load_first_codes(g)
         for c in range(1, COL_BLOCKS):
@@ -170,7 +180,7 @@ def tile_multiheadselfattention_pa_kernel(
         def mx_pass(acc, g, m, c, col0, width):
             nc.tensor.matmul_mx(
                 out=acc,
-                lhsT=x_code[g][:, 2 * P * m : 2 * P * (m + 1)].bitcast(FP4X4),
+                lhsT=(x_head if g == 0 and m < HEAD_TILES else x_code[g])[:, 2 * P * m : 2 * P * (m + 1)].bitcast(FP4X4),
                 lhsT_scale=x_plane[g][:, P * m : P * (m + 1)],
                 rhs=w_code[c][g][:, 2 * col0 : 2 * (col0 + width)].bitcast(FP4X4),
                 rhs_scale=w_plane[c][g][:, col0 : col0 + width],

@@ -251,4 +251,4 @@ def tile_multiheadselfattention_pa_kernel(
             if c < 4:
                 rope(acc[:, :], m, c)
             else:
-                plain(acc[:, :], m, c, col0, width, turn)
+                plain(acc[:, :], m, c, col0, width, turn + 1)

@@ -24,7 +24,8 @@ PAIRS = DH // 2
 
 FLOPS = 2 * TOKENS * D * 3 * H * DH
 
-FIRST_RUNS = ((0, 2), (2, 6), (6, 11), (11, 16))
+X_RUNS = ((0, 2), (2, 5), (5, 8), (8, 12), (12, 16))
+W_RUNS = ((0, 4), (4, 10), (10, 16))
 CHUNK = 4
 WARM_MATMULS = 6
 HEAD_TILES = 4
@@ -52,13 +53,15 @@ def tile_multiheadselfattention_pa_kernel(
         w_code = [[None] * PASSES for c in range(COL_BLOCKS)]
         x_plane_tiles = []
         w_plane_tiles = []
-        for r, (g0, g1) in enumerate(FIRST_RUNS):
+        for r, (g0, g1) in enumerate(X_RUNS):
             xp = keep.tile([P, g1 - g0, TOKENS], U8, name="xp%d" % r, align_bytes=64)
-            wp = keep.tile([P, g1 - g0, N_TILE], U8, name="wp0_%d" % r, align_bytes=64)
             x_plane_tiles.append(xp)
-            w_plane_tiles.append((0, g0, g1, wp))
             for g in range(g0, g1):
                 x_plane[g] = xp[:, g - g0, :]
+        for r, (g0, g1) in enumerate(W_RUNS):
+            wp = keep.tile([P, g1 - g0, N_TILE], U8, name="wp0_%d" % r, align_bytes=64)
+            w_plane_tiles.append((0, g0, g1, wp))
+            for g in range(g0, g1):
                 w_plane[0][g] = wp[:, g - g0, :]
         for g in range(PASSES):
             wc = keep.tile([P, 2 * N_TILE], U8, name="wc0_%d" % g, align_bytes=64)
@@ -81,15 +84,18 @@ def tile_multiheadselfattention_pa_kernel(
         pos_i = keep.tile([P, 2], I32, name="pos_i")
         nc.gpsimd.iota(pos_i[:, :], pattern=[[P, 2]], base=0, channel_multiplier=1)
 
-        for r in range(len(FIRST_RUNS)):
-            nc.vector.memset(x_plane_tiles[r][:, :, :].bitcast(I32), 0)
-            if r > 0:
-                nc.vector.memset(w_plane_tiles[r][3][:, :, :].bitcast(I32), 0)
-        for c, g0, g1, wp in w_plane_tiles[len(FIRST_RUNS):]:
+        for g in range(PASSES):
+            for r, (g0, g1) in enumerate(X_RUNS):
+                if g0 == g:
+                    nc.vector.memset(x_plane_tiles[r][:, :, :].bitcast(I32), 0)
+            for r, (g0, g1) in enumerate(W_RUNS):
+                if g0 == g and r > 0:
+                    nc.vector.memset(w_plane_tiles[r][3][:, :, :].bitcast(I32), 0)
+        for c, g0, g1, wp in w_plane_tiles[len(W_RUNS):]:
             nc.vector.memset(wp[:, :, :].bitcast(I32), 0)
 
         def load_x_scales(r):
-            g0, g1 = FIRST_RUNS[r]
+            g0, g1 = X_RUNS[r]
             for q in range(4):
                 nc.sync.dma_start(
                     out=x_plane_tiles[r][32 * q : 32 * q + 4, :, :].bitcast(I32),
@@ -113,17 +119,21 @@ def tile_multiheadselfattention_pa_kernel(
         head_bytes = 2 * P * HEAD_TILES
         nc.sync.dma_start(out=x_head[:, :].bitcast(I32), in_=x_words[0, :, 0:head_bytes].bitcast(I32))
         nc.sync.dma_start(out=w_code[0][0].bitcast(I32), in_=W_words[0, :, 0 : 2 * N_TILE].bitcast(I32))
-        for r, (g0, g1) in enumerate(FIRST_RUNS):
-            load_w_scales(w_plane_tiles[r])
-            load_x_scales(r)
-            if r == 0:
+        for g in range(PASSES):
+            for r, (g0, g1) in enumerate(W_RUNS):
+                if g0 == g:
+                    load_w_scales(w_plane_tiles[r])
+            for r, (g0, g1) in enumerate(X_RUNS):
+                if g0 == g:
+                    load_x_scales(r)
+            if g == 0:
                 nc.sync.dma_start(
                     out=x_code[0][:, head_bytes:].bitcast(I32), in_=x_words[0, :, head_bytes:].bitcast(I32)
                 )
-            for g in range(max(g0, 1), g1):
+            else:
                 load_first_codes(g)
         for c in range(1, COL_BLOCKS):
-            load_w_scales(w_plane_tiles[len(FIRST_RUNS) + c - 1])
+            load_w_scales(w_plane_tiles[len(W_RUNS) + c - 1])
             for cc, g0, wc in w_chunks:
                 if cc == c:
                     nc.sync.dma_start(

@@ -28,7 +28,7 @@ X_RUNS = ((0, 2), (2, 5), (5, 8), (8, 12), (12, 16))
 W_RUNS = ((0, 4), (4, 10), (10, 16))
 CHUNK = 4
 WARM_MATMULS = 6
-HEAD_TILES = 4
+HEAD_TILES = 2
 
 
 def tile_multiheadselfattention_pa_kernel(

from contextlib import ExitStack
import math

import concourse.mybir as mybir

F32 = mybir.dt.float32
BF16 = mybir.dt.bfloat16
I32 = mybir.dt.int32
U8 = mybir.dt.uint8
FP4X4 = mybir.dt.float4_e2m1fn_x4
ALU = mybir.AluOpType
ACT = mybir.ActivationFunctionType

B, L, D, H, DH = 4, 256, 8192, 16, 64
THETA = 100000.0
P = 128
PASSES = D // 512
TOKENS = B * L
TOKEN_TILES = TOKENS // P
N_TILE = 512
HEADS_PER_BLOCK = N_TILE // DH
COL_BLOCKS = 3 * H * DH // N_TILE
PAIRS = DH // 2

FLOPS = 2 * TOKENS * D * 3 * H * DH

X_RUNS = ((0, 2), (2, 5), (5, 8), (8, 12), (12, 16))
W_RUNS = ((0, 4), (4, 10), (10, 16))
CHUNK = 4
WARM_MATMULS = 6
HEAD_TILES = 2


def tile_multiheadselfattention_pa_kernel(
    tc, x_words, x_scales, W_words, W_scales, out_0, out_1, out_2
):
    nc = tc.nc
    outs = (out_0, out_1, out_2)

    with ExitStack() as ctx:
        keep = ctx.enter_context(tc.tile_pool(name="keep", bufs=1))
        work = ctx.enter_context(tc.tile_pool(name="work", bufs=4))
        psum = ctx.enter_context(tc.psum_pool(name="psum", bufs=8))
        ctx.enter_context(tc.manual_schedule())

        x_code = []
        for g in range(PASSES):
            xc = keep.tile([P, 2 * TOKENS], U8, name="xc%d" % g, align_bytes=64)
            x_code.append(xc)
        x_head = keep.tile([P, 2 * P * HEAD_TILES], U8, name="x_head", align_bytes=64)
        x_plane = [None] * PASSES
        w_plane = [[None] * PASSES for c in range(COL_BLOCKS)]
        w_code = [[None] * PASSES for c in range(COL_BLOCKS)]
        x_plane_tiles = []
        w_plane_tiles = []
        for r, (g0, g1) in enumerate(X_RUNS):
            xp = keep.tile([P, g1 - g0, TOKENS], U8, name="xp%d" % r, align_bytes=64)
            x_plane_tiles.append(xp)
            for g in range(g0, g1):
                x_plane[g] = xp[:, g - g0, :]
        for r, (g0, g1) in enumerate(W_RUNS):
            wp = keep.tile([P, g1 - g0, N_TILE], U8, name="wp0_%d" % r, align_bytes=64)
            w_plane_tiles.append((0, g0, g1, wp))
            for g in range(g0, g1):
                w_plane[0][g] = wp[:, g - g0, :]
        for g in range(PASSES):
            wc = keep.tile([P, 2 * N_TILE], U8, name="wc0_%d" % g, align_bytes=64)
            w_code[0][g] = wc[:, :]
        w_chunks = []
        for c in range(1, COL_BLOCKS):
            wp = keep.tile([P, PASSES, N_TILE], U8, name="wp%d" % c, align_bytes=64)
            w_plane_tiles.append((c, 0, PASSES, wp))
            for g in range(PASSES):
                w_plane[c][g] = wp[:, g, :]
            for g0 in range(0, PASSES, CHUNK):
                wc = keep.tile([P, CHUNK, 2 * N_TILE], U8, name="wc%d_%d" % (c, g0), align_bytes=64)
                w_chunks.append((c, g0, wc))
                for g in range(g0, g0 + CHUNK):
                    w_code[c][g] = wc[:, g - g0, :]

        nc.gpsimd.memset(w_plane_tiles[0][3][:, :, :].bitcast(F32), 0.0)
        warm = keep.tile([P, N_TILE], BF16, name="warm")
        nc.gpsimd.memset(warm[:, :], 0.0)
        pos_i = keep.tile([P, 2], I32, name="pos_i")
        nc.gpsimd.iota(pos_i[:, :], pattern=[[P, 2]], base=0, channel_multiplier=1)

        for g in range(PASSES):
            for r, (g0, g1) in enumerate(X_RUNS):
                if g0 == g:
                    nc.vector.memset(x_plane_tiles[r][:, :, :].bitcast(I32), 0)
            for r, (g0, g1) in enumerate(W_RUNS):
                if g0 == g and r > 0:
                    nc.vector.memset(w_plane_tiles[r][3][:, :, :].bitcast(I32), 0)
        for c, g0, g1, wp in w_plane_tiles[len(W_RUNS):]:
            nc.vector.memset(wp[:, :, :].bitcast(I32), 0)

        def load_x_scales(r):
            g0, g1 = X_RUNS[r]
            for q in range(4):
                nc.sync.dma_start(
                    out=x_plane_tiles[r][32 * q : 32 * q + 4, :, :].bitcast(I32),
                    in_=x_scales[g0:g1, 4 * q : 4 * q + 4, :].rearrange("g r n -> r g n").bitcast(I32),
                )

        def load_w_scales(entry):
            c, g0, g1, wp = entry
            for q in range(4):
                nc.sync.dma_start(
                    out=wp[32 * q : 32 * q + 4, :, :].bitcast(I32),
                    in_=W_scales[g0:g1, 4 * q : 4 * q + 4, c * N_TILE : (c + 1) * N_TILE]
                    .rearrange("g r n -> r g n")
                    .bitcast(I32),
                )

        def load_first_codes(g):
            nc.sync.dma_start(out=x_code[g][:, :].bitcast(I32), in_=x_words[g].bitcast(I32))
            nc.sync.dma_start(out=w_code[0][g].bitcast(I32), in_=W_words[g, :, 0 : 2 * N_TILE].bitcast(I32))

        head_bytes = 2 * P * HEAD_TILES
        nc.sync.dma_start(out=x_head[:, :].bitcast(I32), in_=x_words[0, :, 0:head_bytes].bitcast(I32))
        nc.sync.dma_start(out=w_code[0][0].bitcast(I32), in_=W_words[0, :, 0 : 2 * N_TILE].bitcast(I32))
        for g in range(PASSES):
            for r, (g0, g1) in enumerate(W_RUNS):
                if g0 == g:
                    load_w_scales(w_plane_tiles[r])
            for r, (g0, g1) in enumerate(X_RUNS):
                if g0 == g:
                    load_x_scales(r)
            if g == 0:
                nc.sync.dma_start(
                    out=x_code[0][:, head_bytes:].bitcast(I32), in_=x_words[0, :, head_bytes:].bitcast(I32)
                )
            else:
                load_first_codes(g)
        for c in range(1, COL_BLOCKS):
            load_w_scales(w_plane_tiles[len(W_RUNS) + c - 1])
            for cc, g0, wc in w_chunks:
                if cc == c:
                    nc.sync.dma_start(
                        out=wc[:, :, :].bitcast(I32),
                        in_=W_words[g0 : g0 + CHUNK, :, 2 * N_TILE * c : 2 * N_TILE * (c + 1)]
                        .rearrange("g p n -> p g n")
                        .bitcast(I32),
                    )

        dummy = psum.tile([P, N_TILE], F32, tag="acc", name="dummy")
        for i in range(WARM_MATMULS):
            nc.tensor.matmul(out=dummy[:, :], lhsT=warm[:, 0:P], rhs=warm[:, :], start=True, stop=True)

        pos = keep.tile([P, 2], F32, name="pos")
        nc.vector.tensor_copy(out=pos[:, :], in_=pos_i[:, :])
        t_hi = keep.tile([P, 2, PAIRS], F32, name="t_hi")
        t_lo = keep.tile([P, 2, PAIRS], F32, name="t_lo")
        for i in range(PAIRS):
            turns = THETA ** (-2.0 * i / DH) / (2.0 * math.pi)
            hi = round(turns * 131072.0) / 131072.0
            lo = turns - hi
            nc.vector.tensor_scalar(out=t_hi[:, :, i], in0=pos[:, :], scalar1=hi, scalar2=None, op0=ALU.mult)
            nc.vector.tensor_scalar(out=t_lo[:, :, i], in0=pos[:, :], scalar1=lo, scalar2=None, op0=ALU.mult)
        W2 = 2 * PAIRS
        hi_flat = t_hi[:, :, :].rearrange("p a i -> p (a i)")
        lo_flat = t_lo[:, :, :].rearrange("p a i -> p (a i)")
        k_i = keep.tile([P, W2], I32, name="k_i")
        k_f = keep.tile([P, W2], F32, name="k_f")
        fr = keep.tile([P, W2], F32, name="fr")
        fr1 = keep.tile([P, W2], F32, name="fr1")
        fr2 = keep.tile([P, W2], F32, name="fr2")
        fc = keep.tile([P, W2], F32, name="fc")
        ysn = keep.tile([P, W2], F32, name="ysn")
        ycn = keep.tile([P, W2], F32, name="ycn")
        nc.vector.tensor_copy(out=k_i[:, :], in_=hi_flat)
        nc.vector.tensor_copy(out=k_f[:, :], in_=k_i[:, :])
        nc.vector.tensor_tensor(out=fr[:, :], in0=hi_flat, in1=k_f[:, :], op=ALU.subtract)
        nc.vector.scalar_tensor_tensor(out=fr1[:, :], in0=fr[:, :], scalar=0.0, in1=fr[:, :], op0=ALU.is_lt, op1=ALU.add)
        nc.vector.tensor_tensor(out=fr2[:, :], in0=fr1[:, :], in1=lo_flat, op=ALU.add)
        nc.vector.scalar_tensor_tensor(out=ysn[:, :], in0=fr2[:, :], scalar=0.5, in1=fr2[:, :], op0=ALU.is_gt, op1=ALU.subtract)
        nc.vector.tensor_scalar(out=fc[:, :], in0=fr2[:, :], scalar1=0.25, scalar2=None, op0=ALU.add)
        nc.vector.scalar_tensor_tensor(out=ycn[:, :], in0=fc[:, :], scalar=0.5, in1=fc[:, :], op0=ALU.is_gt, op1=ALU.subtract)

        cos_t = keep.tile([P, 2, PAIRS, 2], F32, name="cos_t")
        sin_t = keep.tile([P, 2, PAIRS, 2], F32, name="sin_t")
        ysn3 = ysn[:, :].rearrange("p (a i) -> p a i", a=2)
        ycn3 = ycn[:, :].rearrange("p (a i) -> p a i", a=2)
        two_pi = 2.0 * math.pi
        nc.scalar.activation(out=sin_t[:, :, :, 0], in_=ysn3, func=ACT.Sin, scale=-two_pi)
        nc.scalar.activation(out=sin_t[:, :, :, 1], in_=ysn3, func=ACT.Sin, scale=two_pi)
        nc.scalar.activation(out=cos_t[:, :, :, 0], in_=ycn3, func=ACT.Sin, scale=-two_pi)
        nc.scalar.activation(out=cos_t[:, :, :, 1], in_=ycn3, func=ACT.Sin, scale=-two_pi)

        def mx_pass(acc, g, m, c, col0, width):
            nc.tensor.matmul_mx(
                out=acc,
                lhsT=(x_head if g == 0 and m < HEAD_TILES else x_code[g])[:, 2 * P * m : 2 * P * (m + 1)].bitcast(FP4X4),
                lhsT_scale=x_plane[g][:, P * m : P * (m + 1)],
                rhs=w_code[c][g][:, 2 * col0 : 2 * (col0 + width)].bitcast(FP4X4),
                rhs_scale=w_plane[c][g][:, col0 : col0 + width],
                start=(g == 0),
                stop=(g == PASSES - 1),
            )

        def dest(m, c, col0, width):
            part = c // 2
            h0 = (c % 2) * HEADS_PER_BLOCK + col0 // DH
            b = m // 2
            l0 = (m % 2) * P
            return outs[part][b, h0 : h0 + width // DH, l0 : l0 + P, :].rearrange("h l d -> l h d")

        def rope(acc, m, c):
            a = m % 2
            heads = HEADS_PER_BLOCK
            cos_b = cos_t[:, a, :, :].rearrange("p i e -> p (i e)").unsqueeze(1).to_broadcast([P, heads, DH])
            sin_b = sin_t[:, a, :, :].rearrange("p i e -> p (i e)").unsqueeze(1).to_broadcast([P, heads, DH])
            acc3 = acc.rearrange("p (h d) -> p h d", h=heads)
            u = work.tile([P, N_TILE], F32, tag="u", bufs=3, name="u")
            nc.scalar.copy(out=u[:, :], in_=acc)
            acc3 = u[:, :].rearrange("p (h d) -> p h d", h=heads)
            t1 = work.tile([P, N_TILE], F32, tag="t1", bufs=6, name="t1")
            t2 = work.tile([P, N_TILE], F32, tag="t2", bufs=3, name="t2")
            nc.vector.tensor_tensor(out=t1[:, :].rearrange("p (h d) -> p h d", h=heads), in0=acc3, in1=cos_b, op=ALU.mult)
            nc.vector.tensor_tensor(out=t2[:, :].rearrange("p (h d) -> p h d", h=heads), in0=acc3, in1=sin_b, op=ALU.mult)
            nc.vector.tensor_tensor(
                out=t1[:, :].rearrange("p (n e) -> p n e", e=2),
                in0=t1[:, :].rearrange("p (n e) -> p n e", e=2),
                in1=t2[:, :].rearrange("p (n e) -> p n e", e=2)[:, :, ::-1],
                op=ALU.add,
            )
            nc.scalar.dma_start(out=dest(m, c, 0, N_TILE), in_=t1[:, :].rearrange("p (h d) -> p h d", h=heads))

        def plain(acc, m, c, col0, width, turn):
            v = work.tile([P, width], F32, tag="v", bufs=4, name="v")
            src = v[:, :].rearrange("p (h d) -> p h d", d=DH)
            if turn % 2 == 0:
                nc.scalar.copy(out=v[:, :], in_=acc)
                nc.scalar.dma_start(out=dest(m, c, col0, width), in_=src)
            else:
                nc.vector.tensor_copy(out=v[:, :], in_=acc)
                nc.sync.dma_start(out=dest(m, c, col0, width), in_=src)

        accs = []
        for m in range(TOKEN_TILES):
            acc = psum.tile([P, N_TILE], F32, tag="acc", name="acc")
            accs.append(acc)
        for g in range(PASSES):
            for m in range(TOKEN_TILES):
                mx_pass(accs[m][:, :], g, m, 0, 0, N_TILE)
        for m in range(TOKEN_TILES):
            rope(accs[m][:, :], m, 0)

        groups = []
        for c in range(1, COL_BLOCKS):
            for m in range(TOKEN_TILES):
                if c == COL_BLOCKS - 1 and m == TOKEN_TILES - 1:
                    groups.append((m, c, 0, N_TILE // 2))
                    groups.append((m, c, N_TILE // 2, N_TILE // 2))
                else:
                    groups.append((m, c, 0, N_TILE))
        for turn, (m, c, col0, width) in enumerate(groups):
            acc = psum.tile([P, width], F32, tag="acc", name="acc")
            for g in range(PASSES):
                mx_pass(acc[:, :], g, m, c, col0, width)
            if c < 4:
                rope(acc[:, :], m, c)
            else:
                plain(acc[:, :], m, c, col0, width, turn + 1)
